import numpy as np
import ml_dtypes


def mxq(x, axis, fmt="e4m3"):
    dtype, down = {"e4m3": (ml_dtypes.float8_e4m3fn, 7), "e5m2": (ml_dtypes.float8_e5m2, 14)}[fmt]
    v = np.moveaxis(np.asarray(x, np.float32).astype(ml_dtypes.bfloat16).astype(np.float64), axis, -1)
    blocks = v.reshape(v.shape[:-1] + (-1, 32))
    amax = np.abs(blocks).max(-1, keepdims=True)
    byte = np.maximum(np.where(amax > 0, np.frexp(amax)[1] - 1 + 127, 0) - down, 1)
    scale = np.exp2(byte - 127.0)
    codes = (blocks / scale).astype(np.float32).astype(dtype).astype(np.float64)
    return np.moveaxis((codes * scale).reshape(v.shape), -1, axis)


WIDE = False


def mx_kscale(k):
    if not WIDE:
        return np.ones(k)
    levels = np.array([10, -10, 5, -5, 0])
    a = np.random.permutation(np.resize(levels, k // 512 * 4)).reshape(k // 512, 4)
    idx = np.arange(k)
    return np.exp2(a[idx // 512, idx % 128 // 32])


BF16 = ml_dtypes.bfloat16


def bf(x):
    return np.asarray(x, np.float32).astype(BF16)


def f64(x):
    return np.asarray(x).astype(np.float64)


B, T, E, C, I, O = 2, 256, 4, 128, 512, 4096


def setup_inputs():
    s = mx_kscale(I)
    return {
        'x': bf((np.random.standard_normal((B, T, E, I)) * s).reshape(B, T, E * I)),
        'combine_array': bf(np.random.uniform(size=(B, T, E, C)) * 4.0 / (C * np.sqrt(E))),
        'dispatch_mask': bf(np.random.uniform(size=(B, T, E, C)) * 1.7 / np.sqrt(T)),
        'weight': bf((np.random.standard_normal((O, E, I)) / np.sqrt(I) / s).reshape(O, E * I)),
        'bias': bf(np.random.standard_normal(O) * 0.25),
        'num_experts': E,
    }


def reference(x, combine_array, dispatch_mask, weight, bias, num_experts):
    x, combine_array, dispatch_mask, weight, bias = f64(x), f64(combine_array), f64(dispatch_mask), f64(weight), f64(bias)
    e = num_experts
    i = weight.shape[1] // e
    w = weight.reshape(e, -1, i)
    b = x.shape[0]
    xr = x.reshape(b, -1, e, i)
    xd = dispatch_mask.transpose(0, 2, 3, 1) @ xr.transpose(0, 2, 1, 3)
    y = (mxq(xd, 3, 'e4m3') @ mxq(w, 2, 'e4m3').transpose(0, 2, 1)) + bias
    k = e * y.shape[2]
    return mxq(combine_array.reshape(b, -1, k), 2, 'e4m3') @ mxq(y.reshape(b, k, -1), 1, 'e4m3')

@@ -1,0 +1,253 @@
+from contextlib import ExitStack
+
+import concourse.mybir as mybir
+from concourse.masks import make_identity
+
+F32 = mybir.dt.float32
+BF16 = mybir.dt.bfloat16
+U32 = mybir.dt.uint32
+U8 = mybir.dt.uint8
+FP8X4 = mybir.dt.float8_e4m3fn_x4
+ADD = mybir.AluOpType.add
+
+B, T, E, C, I, O = 2, 256, 4, 128, 512, 4096
+P = 128
+OC = 512
+NCH = O // OC
+FLOPS = 2 * B * E * C * I * T + 2 * B * E * C * I * O + 2 * B * T * E * C * O
+MANUAL = False
+
+
+def tile_expertschoosemaskedexpand_kernel(
+    tc, x, combine_array, dispatch_mask, weight, bias, num_experts, out
+):
+    nc = tc.nc
+    with ExitStack() as ctx:
+        const = ctx.enter_context(tc.tile_pool(name="const", bufs=1))
+        wraw_pool = ctx.enter_context(tc.tile_pool(name="wraw", bufs=3))
+        wg_pool = ctx.enter_context(tc.tile_pool(name="wg", bufs=6))
+        wq_pool = ctx.enter_context(tc.tile_pool(name="wq", bufs=10))
+        yg_pool = ctx.enter_context(tc.tile_pool(name="yg", bufs=2))
+        yq_pool = ctx.enter_context(tc.tile_pool(name="yq", bufs=3))
+        o_pool = ctx.enter_context(tc.tile_pool(name="osb", bufs=3))
+        ps_t = ctx.enter_context(tc.psum_pool(name="ps_t", bufs=3))
+        ps_y = ctx.enter_context(tc.psum_pool(name="ps_y", bufs=3))
+        ps_o = ctx.enter_context(tc.psum_pool(name="ps_o", bufs=2))
+        if MANUAL:
+            ctx.enter_context(tc.manual_schedule())
+
+        ident_f = const.tile([P, P], F32, name="ident_f")
+        make_identity(nc, ident_f[:])
+        ident_b = const.tile([P, P], BF16, name="ident_b")
+        make_identity(nc, ident_b[:])
+
+        w_view = weight.rearrange("(e c p) f -> c p e f", e=E, c=NCH, p=P)
+        x_sb, dm_sb = [], []
+        for b in range(B):
+            x_sb.append(const.tile([P, 2, E * I], BF16, name="x_sb%d" % b))
+            dm_sb.append(const.tile([P, 2, E * C], BF16, name="dm_sb%d" % b))
+        comb_sb = const.tile([P, 2 * B, E * C], BF16, name="comb_sb")
+        bias_a = const.tile([P, 2 * OC], BF16, name="bias_a")
+        bias_b = const.tile([P, O - 2 * OC], BF16, name="bias_b")
+        wraw = {}
+
+        def load_xb(b):
+            nc.sync.dma_start(
+                out=dm_sb[b][:], in_=dispatch_mask[b].rearrange("(h p) e c -> p h (e c)", p=P)
+            )
+            nc.sync.dma_start(out=x_sb[b][:], in_=x[b].rearrange("(h p) f -> p h f", p=P))
+
+        def load_w(n, sliced):
+            if sliced:
+                wr = wraw_pool.tile([P, 4, E, I], BF16, name="wr", tag="wr")
+                for s in range(4):
+                    nc.sync.dma_start(out=wr[:, s], in_=w_view[n][:, :, s * I : (s + 1) * I])
+            else:
+                wr = wraw_pool.tile([P, E, 4, I], BF16, name="wr", tag="wr")
+                nc.sync.dma_start(
+                    out=wr[:].rearrange("p e s i -> p e (s i)"), in_=w_view[n]
+                )
+            wraw[n] = (wr, sliced)
+
+        def w_words(n, s, e):
+            wr, sliced = wraw[n]
+            rows = wr[:, s, e, :] if sliced else wr[:, e, s, :]
+            return rows.bitcast(F32)
+
+        load_xb(0)
+        load_w(0, True)
+        nc.sync.dma_start(out=bias_a[:], in_=bias[0 : 2 * OC].partition_broadcast(P))
+        load_xb(1)
+        load_w(1, True)
+        nc.sync.dma_start(
+            out=comb_sb[:], in_=combine_array.rearrange("b (h p) e c -> p (b h) (e c)", p=P)
+        )
+        nc.sync.dma_start(out=bias_b[:], in_=bias[2 * OC : O].partition_broadcast(P))
+
+        x_codes, x_scales = [], []
+
+        def step1(b):
+            xg = const.tile([P, E, C, 4], BF16, name="xg%d" % b, align_bytes=64)
+            for e in range(E):
+                xp = ps_y.tile([P, 4, C], F32, name="xp", tag="yp")
+                for u in range(2):
+                    for w in range(2):
+                        for h in range(2):
+                            cols = x_sb[b][:, h, e * I : (e + 1) * I].rearrange(
+                                "t (u q w) -> t u w q", u=2, w=2
+                            )
+                            nc.tensor.matmul(
+                                out=xp[:, 2 * u + w, :],
+                                lhsT=cols[:, u, w, :],
+                                rhs=dm_sb[b][:, h, e * C : (e + 1) * C],
+                                start=(h == 0),
+                                stop=(h == 1),
+                            )
+                nc.scalar.copy(out=xg[:, e], in_=xp[:].rearrange("q t c -> q c t"))
+            xc = const.tile([P, E * C], U32, name="xc%d" % b, align_bytes=64)
+            xs = const.tile([P, E * C], U8, name="xs%d" % b, align_bytes=64)
+            nc.vector.quantize_mx(
+                out=xc[:].bitcast(FP8X4),
+                scales=xs[:],
+                in_=xg[:].rearrange("q e c t -> q (e c t)"),
+            )
+            x_codes.append(xc)
+            x_scales.append(xs)
+
+        cg = const.tile([P, 2 * B, P, 4], BF16, name="cg", align_bytes=64)
+        c_codes = const.tile([P, 2 * B * P], U32, name="c_codes", align_bytes=64)
+        c_scales = const.tile([P, 2 * B * P], U8, name="c_scales", align_bytes=64)
+
+        def comb_prep():
+            for bh in range(2 * B):
+                cp = ps_o.tile([P, E, P], BF16, name="cp", tag="op")
+                for e in range(E):
+                    nc.tensor.transpose(
+                        cp[:, e, :], comb_sb[:, bh, e * C : (e + 1) * C], ident_b[:]
+                    )
+                nc.scalar.copy(out=cg[:, bh], in_=cp[:].rearrange("c e t -> c t e"))
+            nc.vector.quantize_mx(
+                out=c_codes[:].bitcast(FP8X4),
+                scales=c_scales[:],
+                in_=cg[:].rearrange("c g t e -> c (g t e)"),
+            )
+
+        wg_t, w_codes, w_scales = {}, {}, {}
+
+        def trans(n, s):
+            wg = wg_pool.tile([P, 4 * E * P], BF16, name="wg", tag="wg", align_bytes=64)
+            wgf = wg[:].bitcast(F32).rearrange("q (n u) -> q n u", u=2)
+            for ep in range(2):
+                tp = ps_t.tile([P, 2, 2 * P], F32, name="tp", tag="tp")
+                for el in range(2):
+                    words = w_words(n, s, 2 * ep + el)
+                    for u in range(2):
+                        nc.tensor.transpose(
+                            tp[:, u, el * P : (el + 1) * P],
+                            words[:, u * P : (u + 1) * P],
+                            ident_f[:],
+                        )
+                nc.scalar.copy(
+                    out=wgf[:, ep * 2 * P : (ep + 1) * 2 * P, :],
+                    in_=tp[:].rearrange("q u n -> q n u"),
+                )
+            wg_t[(n, s)] = wg
+
+        def qw(n, s):
+            wc = wq_pool.tile([P, E * P], U32, name="wc", tag="wc", align_bytes=64)
+            ws = wq_pool.tile([P, E * P], U8, name="ws", tag="ws", align_bytes=64)
+            nc.vector.quantize_mx(out=wc[:].bitcast(FP8X4), scales=ws[:], in_=wg_t[(n, s)][:])
+            w_codes[(n, s)] = wc
+            w_scales[(n, s)] = ws
+
+        yg_t, y_codes, y_scales, o_t = {}, {}, {}, {}
+
+        def s2(n, b, s):
+            if s == 0:
+                yg_t[(n, b)] = yg_pool.tile([P, OC, E], BF16, name="yg", tag="yg", align_bytes=64)
+            yp = ps_y.tile([P, E, P], F32, name="yp", tag="yp")
+            for e in range(E):
+                nc.tensor.matmul_mx(
+                    out=yp[:, e, :],
+                    lhsT=x_codes[b][:, e * C : (e + 1) * C].bitcast(FP8X4),
+                    lhsT_scale=x_scales[b][:, e * C : (e + 1) * C],
+                    rhs=w_codes[(n, s)][:, e * P : (e + 1) * P].bitcast(FP8X4),
+                    rhs_scale=w_scales[(n, s)][:, e * P : (e + 1) * P],
+                    start=True,
+                    stop=True,
+                )
+            if n < 2:
+                bsrc = bias_a[:, n * OC : (n + 1) * OC]
+            else:
+                bsrc = bias_b[:, (n - 2) * OC : (n - 1) * OC]
+            bcol = bsrc.rearrange("c (p j) -> c j p", j=4)[:, s, :]
+            nc.vector.tensor_tensor(
+                out=yg_t[(n, b)][:, s * P : (s + 1) * P, :],
+                in0=yp[:].rearrange("c e p -> c p e"),
+                in1=bcol.unsqueeze(2).to_broadcast([P, P, E]),
+                op=ADD,
+            )
+
+        def qy(n, b):
+            yc = yq_pool.tile([P, OC], U32, name="yc", tag="yc", align_bytes=64)
+            ys = yq_pool.tile([P, OC], U8, name="ys", tag="ys", align_bytes=64)
+            nc.vector.quantize_mx(
+                out=yc[:].bitcast(FP8X4),
+                scales=ys[:],
+                in_=yg_t[(n, b)][:].rearrange("c n e -> c (n e)"),
+            )
+            y_codes[(n, b)] = yc
+            y_scales[(n, b)] = ys
+
+        def s3(n, b):
+            osb = o_pool.tile([P, 2, OC], F32, name="osb", tag="osb")
+            for h in range(2):
+                bh = 2 * b + h
+                op = ps_o.tile([P, OC], F32, name="op", tag="op")
+                nc.tensor.matmul_mx(
+                    out=op[:],
+                    lhsT=c_codes[:, bh * P : (bh + 1) * P].bitcast(FP8X4),
+                    lhsT_scale=c_scales[:, bh * P : (bh + 1) * P],
+                    rhs=y_codes[(n, b)][:].bitcast(FP8X4),
+                    rhs_scale=y_scales[(n, b)][:],
+                    start=True,
+                    stop=True,
+                )
+                nc.scalar.copy(
+                    out=osb[:, h, :].rearrange("t (p s) -> t p s", s=4),
+                    in_=op[:].rearrange("t (s p) -> t p s", s=4),
+                )
+            nc.scalar.dma_start(
+                out=out[b, :, n * OC : (n + 1) * OC].rearrange("(h p) o -> p h o", p=P),
+                in_=osb[:],
+            )
+
+        step1(0)
+        for s in range(4):
+            trans(0, s)
+            qw(0, s)
+            s2(0, 0, s)
+        qy(0, 0)
+        step1(1)
+        comb_prep()
+        periods = [(n, b) for n in range(NCH) for b in range(B)]
+        done_t = 4
+        done_q = 4
+        for k in range(1, len(periods)):
+            n, b = periods[k]
+            if b == 1 and n + 2 < NCH:
+                load_w(n + 2, False)
+            for s in range(4):
+                s2(n, b, s)
+            pn, pb = periods[k - 1]
+            s3(pn, pb)
+            want_t = min(4 * NCH, 2 * (k + 3))
+            while done_t < want_t:
+                trans(done_t // 4, done_t % 4)
+                done_t += 1
+            want_q = min(4 * NCH, 2 * (k + 3))
+            while done_q < want_q:
+                qw(done_q // 4, done_q % 4)
+                done_q += 1
+            qy(n, b)
+        s3(NCH - 1, 1)

@@ -15,7 +15,17 @@ P = 128
 OC = 512
 NCH = O // OC
 FLOPS = 2 * B * E * C * I * T + 2 * B * E * C * I * O + 2 * B * T * E * C * O
-MANUAL = False
+MANUAL = True
+TP_BUFS, YP_BUFS, OP_BUFS = 3, 3, 2
+PARTS = [4, 4, 2]
+LOADS = [("x", 0), ("x", 1), ("w", 0, 0), "ba", ("w", 0, 1), ("w", 0, 2), ("w", 0, 3), "c",
+         ("w", 1, None), ("w", 2, 0), "bb", ("w", 2, 1)]
+LT = 3
+LQ = 1
+HEAD = 8
+COMB_AT = 2
+QC_AT = 3
+WRAW_BUFS, WG_BUFS, WQ_BUFS, YQ_BUFS, O_BUFS = 3, 6, 8, 6, 3
 
 
 def tile_expertschoosemaskedexpand_kernel(
@@ -24,15 +34,15 @@ def tile_expertschoosemaskedexpand_kernel(
     nc = tc.nc
     with ExitStack() as ctx:
         const = ctx.enter_context(tc.tile_pool(name="const", bufs=1))
-        wraw_pool = ctx.enter_context(tc.tile_pool(name="wraw", bufs=3))
-        wg_pool = ctx.enter_context(tc.tile_pool(name="wg", bufs=6))
-        wq_pool = ctx.enter_context(tc.tile_pool(name="wq", bufs=10))
-        yg_pool = ctx.enter_context(tc.tile_pool(name="yg", bufs=2))
-        yq_pool = ctx.enter_context(tc.tile_pool(name="yq", bufs=3))
-        o_pool = ctx.enter_context(tc.tile_pool(name="osb", bufs=3))
-        ps_t = ctx.enter_context(tc.psum_pool(name="ps_t", bufs=3))
-        ps_y = ctx.enter_context(tc.psum_pool(name="ps_y", bufs=3))
-        ps_o = ctx.enter_context(tc.psum_pool(name="ps_o", bufs=2))
+        wraw_pool = ctx.enter_context(tc.tile_pool(name="wraw", bufs=WRAW_BUFS))
+        wg_pool = ctx.enter_context(tc.tile_pool(name="wg", bufs=WG_BUFS))
+        wq_pool = ctx.enter_context(tc.tile_pool(name="wq", bufs=WQ_BUFS))
+        yg_pool = ctx.enter_context(tc.tile_pool(name="yg", bufs=4))
+        yq_pool = ctx.enter_context(tc.tile_pool(name="yq", bufs=YQ_BUFS))
+        o_pool = ctx.enter_context(tc.tile_pool(name="osb", bufs=O_BUFS))
+        ps_t = ctx.enter_context(tc.psum_pool(name="ps_t", bufs=TP_BUFS))
+        ps_y = ctx.enter_context(tc.psum_pool(name="ps_y", bufs=YP_BUFS))
+        ps_o = ctx.enter_context(tc.psum_pool(name="ps_o", bufs=OP_BUFS))
         if MANUAL:
             ctx.enter_context(tc.manual_schedule())
 
@@ -57,101 +67,116 @@ def tile_expertschoosemaskedexpand_kernel(
             )
             nc.sync.dma_start(out=x_sb[b][:], in_=x[b].rearrange("(h p) f -> p h f", p=P))
 
-        def load_w(n, sliced):
-            if sliced:
-                wr = wraw_pool.tile([P, 4, E, I], BF16, name="wr", tag="wr")
-                for s in range(4):
-                    nc.sync.dma_start(out=wr[:, s], in_=w_view[n][:, :, s * I : (s + 1) * I])
-            else:
-                wr = wraw_pool.tile([P, E, 4, I], BF16, name="wr", tag="wr")
+        def load_w(n, part=None):
+            parts = PARTS[n] if n < len(PARTS) else 1
+            per = 4 // parts
+            if part is None or part == 0:
+                wraw[n] = (wraw_pool.tile([P, parts, E, per * I], BF16, name="wr", tag="wr"), per)
+            wr = wraw[n][0]
+            for g in range(parts) if part is None else [part]:
                 nc.sync.dma_start(
-                    out=wr[:].rearrange("p e s i -> p e (s i)"), in_=w_view[n]
+                    out=wr[:, g], in_=w_view[n][:, :, g * per * I : (g + 1) * per * I]
                 )
-            wraw[n] = (wr, sliced)
 
         def w_words(n, s, e):
-            wr, sliced = wraw[n]
-            rows = wr[:, s, e, :] if sliced else wr[:, e, s, :]
+            wr, per = wraw[n]
+            rows = wr[:, s // per, e, (s % per) * I : (s % per + 1) * I]
             return rows.bitcast(F32)
 
-        load_xb(0)
-        load_w(0, True)
-        nc.sync.dma_start(out=bias_a[:], in_=bias[0 : 2 * OC].partition_broadcast(P))
-        load_xb(1)
-        load_w(1, True)
-        nc.sync.dma_start(
-            out=comb_sb[:], in_=combine_array.rearrange("b (h p) e c -> p (b h) (e c)", p=P)
-        )
-        nc.sync.dma_start(out=bias_b[:], in_=bias[2 * OC : O].partition_broadcast(P))
+        def load(tok):
+            if tok == "ba":
+                nc.sync.dma_start(out=bias_a[:], in_=bias[0 : 2 * OC].partition_broadcast(P))
+            elif tok == "bb":
+                nc.sync.dma_start(out=bias_b[:], in_=bias[2 * OC : O].partition_broadcast(P))
+            elif tok == "c":
+                nc.sync.dma_start(
+                    out=comb_sb[:],
+                    in_=combine_array.rearrange("b (h p) e c -> p (b h) (e c)", p=P),
+                )
+            elif tok[0] == "x":
+                load_xb(tok[1])
+            else:
+                load_w(tok[1], tok[2])
 
-        x_codes, x_scales = [], []
+        for tok in LOADS:
+            load(tok)
 
-        def step1(b):
-            xg = const.tile([P, E, C, 4], BF16, name="xg%d" % b, align_bytes=64)
-            for e in range(E):
-                xp = ps_y.tile([P, 4, C], F32, name="xp", tag="yp")
-                for u in range(2):
-                    for w in range(2):
-                        for h in range(2):
-                            cols = x_sb[b][:, h, e * I : (e + 1) * I].rearrange(
-                                "t (u q w) -> t u w q", u=2, w=2
-                            )
-                            nc.tensor.matmul(
-                                out=xp[:, 2 * u + w, :],
-                                lhsT=cols[:, u, w, :],
-                                rhs=dm_sb[b][:, h, e * C : (e + 1) * C],
-                                start=(h == 0),
-                                stop=(h == 1),
-                            )
-                nc.scalar.copy(out=xg[:, e], in_=xp[:].rearrange("q t c -> q c t"))
+        xg_t, x_codes, x_scales = {}, {}, {}
+
+        def step1(b, e):
+            if e == 0:
+                xg_t[b] = const.tile([P, E, C, 4], BF16, name="xg%d" % b, align_bytes=64)
+            xp = ps_y.tile([P, 4, C], F32, name="xp", tag="yp")
+            for u in range(2):
+                for w in range(2):
+                    for h in range(2):
+                        cols = x_sb[b][:, h, e * I : (e + 1) * I].rearrange(
+                            "t (u q w) -> t u w q", u=2, w=2
+                        )
+                        nc.tensor.matmul(
+                            out=xp[:, 2 * u + w, :],
+                            lhsT=cols[:, u, w, :],
+                            rhs=dm_sb[b][:, h, e * C : (e + 1) * C],
+                            start=(h == 0),
+                            stop=(h == 1),
+                        )
+            nc.scalar.copy(out=xg_t[b][:, e], in_=xp[:].rearrange("q t c -> q c t"))
+
+        def qx(b):
             xc = const.tile([P, E * C], U32, name="xc%d" % b, align_bytes=64)
             xs = const.tile([P, E * C], U8, name="xs%d" % b, align_bytes=64)
             nc.vector.quantize_mx(
                 out=xc[:].bitcast(FP8X4),
                 scales=xs[:],
-                in_=xg[:].rearrange("q e c t -> q (e c t)"),
+                in_=xg_t[b][:].rearrange("q e c t -> q (e c t)"),
             )
-            x_codes.append(xc)
-            x_scales.append(xs)
+            x_codes[b] = xc
+            x_scales[b] = xs
 
         cg = const.tile([P, 2 * B, P, 4], BF16, name="cg", align_bytes=64)
         c_codes = const.tile([P, 2 * B * P], U32, name="c_codes", align_bytes=64)
         c_scales = const.tile([P, 2 * B * P], U8, name="c_scales", align_bytes=64)
 
-        def comb_prep():
-            for bh in range(2 * B):
-                cp = ps_o.tile([P, E, P], BF16, name="cp", tag="op")
+        def comb_t(b):
+            cp = ps_o.tile([P, 2, E, P], BF16, name="cp", tag="op")
+            for hh in range(2):
                 for e in range(E):
                     nc.tensor.transpose(
-                        cp[:, e, :], comb_sb[:, bh, e * C : (e + 1) * C], ident_b[:]
+                        cp[:, hh, e, :], comb_sb[:, 2 * b + hh, e * C : (e + 1) * C], ident_b[:]
                     )
-                nc.scalar.copy(out=cg[:, bh], in_=cp[:].rearrange("c e t -> c t e"))
+            nc.scalar.copy(
+                out=cg[:, 2 * b : 2 * b + 2], in_=cp[:].rearrange("c g e t -> c g t e")
+            )
+
+        def qc():
             nc.vector.quantize_mx(
                 out=c_codes[:].bitcast(FP8X4),
                 scales=c_scales[:],
                 in_=cg[:].rearrange("c g t e -> c (g t e)"),
             )
 
-        wg_t, w_codes, w_scales = {}, {}, {}
+        tp_t, wg_t, w_codes, w_scales = {}, {}, {}, {}
 
-        def trans(n, s):
-            wg = wg_pool.tile([P, 4 * E * P], BF16, name="wg", tag="wg", align_bytes=64)
-            wgf = wg[:].bitcast(F32).rearrange("q (n u) -> q n u", u=2)
-            for ep in range(2):
-                tp = ps_t.tile([P, 2, 2 * P], F32, name="tp", tag="tp")
-                for el in range(2):
-                    words = w_words(n, s, 2 * ep + el)
-                    for u in range(2):
-                        nc.tensor.transpose(
-                            tp[:, u, el * P : (el + 1) * P],
-                            words[:, u * P : (u + 1) * P],
-                            ident_f[:],
-                        )
-                nc.scalar.copy(
-                    out=wgf[:, ep * 2 * P : (ep + 1) * 2 * P, :],
-                    in_=tp[:].rearrange("q u n -> q n u"),
+        def t_pe(n, s, ep):
+            tp = ps_t.tile([P, 2, 2 * P], F32, name="tp", tag="tp")
+            for el in range(2):
+                words = w_words(n, s, 2 * ep + el)
+                for u in range(2):
+                    nc.tensor.transpose(
+                        tp[:, u, el * P : (el + 1) * P], words[:, u * P : (u + 1) * P], ident_f[:]
+                    )
+            tp_t[(n, s, ep)] = tp
+
+        def t_ev(n, s, ep):
+            if ep == 0:
+                wg_t[(n, s)] = wg_pool.tile(
+                    [P, 4 * E * P], BF16, name="wg", tag="wg", align_bytes=64
                 )
-            wg_t[(n, s)] = wg
+            wgf = wg_t[(n, s)][:].bitcast(F32).rearrange("q (n u) -> q n u", u=2)
+            nc.scalar.copy(
+                out=wgf[:, ep * 2 * P : (ep + 1) * 2 * P, :],
+                in_=tp_t[(n, s, ep)][:].rearrange("q u n -> q n u"),
+            )
 
         def qw(n, s):
             wc = wq_pool.tile([P, E * P], U32, name="wc", tag="wc", align_bytes=64)
@@ -160,11 +185,9 @@ def tile_expertschoosemaskedexpand_kernel(
             w_codes[(n, s)] = wc
             w_scales[(n, s)] = ws
 
-        yg_t, y_codes, y_scales, o_t = {}, {}, {}, {}
+        yp_t, yg_t, y_codes, y_scales, op_t, o_t = {}, {}, {}, {}, {}, {}
 
-        def s2(n, b, s):
-            if s == 0:
-                yg_t[(n, b)] = yg_pool.tile([P, OC, E], BF16, name="yg", tag="yg", align_bytes=64)
+        def s2_pe(n, b, s):
             yp = ps_y.tile([P, E, P], F32, name="yp", tag="yp")
             for e in range(E):
                 nc.tensor.matmul_mx(
@@ -176,6 +199,11 @@ def tile_expertschoosemaskedexpand_kernel(
                     start=True,
                     stop=True,
                 )
+            yp_t[(n, b, s)] = yp
+
+        def ye(n, b, s):
+            if s == 0:
+                yg_t[(n, b)] = yg_pool.tile([P, OC, E], BF16, name="yg", tag="yg", align_bytes=64)
             if n < 2:
                 bsrc = bias_a[:, n * OC : (n + 1) * OC]
             else:
@@ -183,71 +211,142 @@ def tile_expertschoosemaskedexpand_kernel(
             bcol = bsrc.rearrange("c (p j) -> c j p", j=4)[:, s, :]
             nc.vector.tensor_tensor(
                 out=yg_t[(n, b)][:, s * P : (s + 1) * P, :],
-                in0=yp[:].rearrange("c e p -> c p e"),
+                in0=yp_t[(n, b, s)][:].rearrange("c e p -> c p e"),
                 in1=bcol.unsqueeze(2).to_broadcast([P, P, E]),
                 op=ADD,
             )
 
-        def qy(n, b):
-            yc = yq_pool.tile([P, OC], U32, name="yc", tag="yc", align_bytes=64)
-            ys = yq_pool.tile([P, OC], U8, name="ys", tag="ys", align_bytes=64)
+        def qy(n, b, half):
+            if half == 0:
+                y_codes[(n, b)] = yq_pool.tile([P, OC], U32, name="yc", tag="yc", align_bytes=64)
+                y_scales[(n, b)] = yq_pool.tile([P, OC], U8, name="ys", tag="ys", align_bytes=64)
+            cols = slice(half * 2 * P, (half + 1) * 2 * P)
             nc.vector.quantize_mx(
-                out=yc[:].bitcast(FP8X4),
-                scales=ys[:],
-                in_=yg_t[(n, b)][:].rearrange("c n e -> c (n e)"),
+                out=y_codes[(n, b)][:, cols].bitcast(FP8X4),
+                scales=y_scales[(n, b)][:, cols],
+                in_=yg_t[(n, b)][:, cols, :].rearrange("c n e -> c (n e)"),
             )
-            y_codes[(n, b)] = yc
-            y_scales[(n, b)] = ys
 
-        def s3(n, b):
-            osb = o_pool.tile([P, 2, OC], F32, name="osb", tag="osb")
-            for h in range(2):
-                bh = 2 * b + h
-                op = ps_o.tile([P, OC], F32, name="op", tag="op")
-                nc.tensor.matmul_mx(
-                    out=op[:],
-                    lhsT=c_codes[:, bh * P : (bh + 1) * P].bitcast(FP8X4),
-                    lhsT_scale=c_scales[:, bh * P : (bh + 1) * P],
-                    rhs=y_codes[(n, b)][:].bitcast(FP8X4),
-                    rhs_scale=y_scales[(n, b)][:],
-                    start=True,
-                    stop=True,
-                )
-                nc.scalar.copy(
-                    out=osb[:, h, :].rearrange("t (p s) -> t p s", s=4),
-                    in_=op[:].rearrange("t (s p) -> t p s", s=4),
-                )
+        def s3_pe(n, b, h):
+            bh = 2 * b + h
+            op = ps_o.tile([P, OC], F32, name="op", tag="op")
+            nc.tensor.matmul_mx(
+                out=op[:],
+                lhsT=c_codes[:, bh * P : (bh + 1) * P].bitcast(FP8X4),
+                lhsT_scale=c_scales[:, bh * P : (bh + 1) * P],
+                rhs=y_codes[(n, b)][:].bitcast(FP8X4),
+                rhs_scale=y_scales[(n, b)][:],
+                start=True,
+                stop=True,
+            )
+            op_t[(n, b, h)] = op
+
+        def o_ev(n, b, h, eng):
+            if h == 0:
+                o_t[(n, b)] = o_pool.tile([P, 2, OC], F32, name="osb", tag="osb")
+            dst = o_t[(n, b)][:, h, :].rearrange("t (p s) -> t p s", s=4)
+            src = op_t[(n, b, h)][:].rearrange("t (s p) -> t p s", s=4)
+            if eng == 0:
+                nc.scalar.copy(out=dst, in_=src)
+            else:
+                nc.vector.tensor_copy(out=dst, in_=src)
+
+        def store(n, b):
             nc.scalar.dma_start(
                 out=out[b, :, n * OC : (n + 1) * OC].rearrange("(h p) o -> p h o", p=P),
-                in_=osb[:],
+                in_=o_t[(n, b)][:],
             )
 
-        step1(0)
-        for s in range(4):
-            trans(0, s)
-            qw(0, s)
-            s2(0, 0, s)
-        qy(0, 0)
-        step1(1)
-        comb_prep()
-        periods = [(n, b) for n in range(NCH) for b in range(B)]
-        done_t = 4
-        done_q = 4
-        for k in range(1, len(periods)):
-            n, b = periods[k]
-            if b == 1 and n + 2 < NCH:
-                load_w(n + 2, False)
-            for s in range(4):
-                s2(n, b, s)
-            pn, pb = periods[k - 1]
-            s3(pn, pb)
-            want_t = min(4 * NCH, 2 * (k + 3))
-            while done_t < want_t:
-                trans(done_t // 4, done_t % 4)
-                done_t += 1
-            want_q = min(4 * NCH, 2 * (k + 3))
-            while done_q < want_q:
-                qw(done_q // 4, done_q % 4)
-                done_q += 1
-            qy(n, b)
-        s3(NCH - 1, 1)
+        NSL = 4 * NCH
+        state = {"t": 0, "q": 0, "w": 3, "s3": 0}
+        s3_todo = []
+
+        def t_upto(want):
+            want = min(NSL, want)
+            banks = [(sl // 4, sl % 4, ep) for sl in range(state["t"], want) for ep in range(2)]
+            for i, bk in enumerate(banks):
+                if i >= TP_BUFS:
+                    t_ev(*banks[i - TP_BUFS])
+                if bk[1] == 0 and bk[2] == 0 and bk[0] >= 1 and state["w"] < NCH:
+                    load_w(state["w"])
+                    state["w"] += 1
+                t_pe(*bk)
+            for bk in banks[max(0, len(banks) - TP_BUFS) :]:
+                t_ev(*bk)
+            state["t"] = max(state["t"], want)
+
+        def q_upto(want):
+            want = min(NSL, want)
+            while state["q"] < want:
+                qw(state["q"] // 4, state["q"] % 4)
+                state["q"] += 1
+
+        def s3_some(count):
+            for j in range(count):
+                if state["s3"] < len(s3_todo):
+                    n, b, hh = s3_todo[state["s3"]]
+                    state["s3"] += 1
+                    s3_pe(n, b, hh)
+                    o_ev(n, b, hh, 0)
+                    if hh == 1:
+                        store(n, b)
+
+        def group(a, z):
+            more = 0 if z < HEAD else 1
+            units = [(sl // 4, b, sl % 4) for sl in range(a, z) for b in range(B)]
+            nu = len(units)
+            q_at = nu // 2 if nu > 2 else 0
+            seen = [0]
+
+            def v_step():
+                if seen[0] == q_at:
+                    q_upto(z + LQ + more)
+                ye(*units[seen[0]])
+                seen[0] += 1
+
+            for i, un in enumerate(units):
+                if i == min(YP_BUFS, nu - 1) and a > QC_AT:
+                    backlog = len(s3_todo) - state["s3"]
+                    s3_some((z - a) + (1 if backlog > 4 else 0))
+                if i >= YP_BUFS:
+                    v_step()
+                s2_pe(*un)
+            for b in range(B):
+                if a <= COMB_AT + b < z:
+                    comb_t(b)
+            t_upto(z + LT + more)
+            while seen[0] < nu:
+                v_step()
+            if a <= QC_AT < z:
+                qc()
+            if z % 2 == 0:
+                n, half = (z - 1) // 4, ((z - 1) % 4) // 2
+                for b in range(B):
+                    qy(n, b, half)
+                if half == 1:
+                    s3_todo.extend([(n, b, hh) for b in range(B) for hh in range(2)])
+
+        for b in range(B):
+            for e in range(E):
+                step1(b, e)
+            qx(b)
+        t_upto(LT)
+        q_upto(LQ)
+        a = 0
+        while a < NSL:
+            z = a + (1 if a < HEAD else 2)
+            group(a, z)
+            a = z
+        rest = s3_todo[state["s3"] :]
+        for i, (n, b, hh) in enumerate(rest):
+            if i >= OP_BUFS:
+                pn, pb, ph = rest[i - OP_BUFS]
+                o_ev(pn, pb, ph, (i - OP_BUFS) % 2)
+                if ph == 1:
+                    store(pn, pb)
+            s3_pe(n, b, hh)
+        for i in range(max(0, len(rest) - OP_BUFS), len(rest)):
+            n, b, hh = rest[i]
+            o_ev(n, b, hh, i % 2)
+            if hh == 1:
+                store(n, b)

@@ -210,9 +210,11 @@ def tile_expertschoosemaskedexpand_kernel(
                 bsrc = bias_b[:, (n - 2) * OC : (n - 1) * OC]
             bcol = bsrc.rearrange("c (p j) -> c j p", j=4)[:, s, :]
             nc.vector.tensor_tensor(
-                out=yg_t[(n, b)][:, s * P : (s + 1) * P, :],
-                in0=yp_t[(n, b, s)][:].rearrange("c e p -> c p e"),
-                in1=bcol.unsqueeze(2).to_broadcast([P, P, E]),
+                out=yg_t[(n, b)][:, s * P : (s + 1) * P, :].rearrange("c (g i) e -> c g e i", i=4),
+                in0=yp_t[(n, b, s)][:].rearrange("c e (g i) -> c g e i", i=4),
+                in1=bcol.rearrange("c (g i) -> c g i", i=4)
+                .unsqueeze(2)
+                .to_broadcast([P, P // 4, E, 4]),
                 op=ADD,
             )
 

@@ -18,13 +18,13 @@ FLOPS = 2 * B * E * C * I * T + 2 * B * E * C * I * O + 2 * B * T * E * C * O
 MANUAL = True
 TP_BUFS, YP_BUFS, OP_BUFS = 3, 3, 2
 PARTS = [4, 4, 2]
-LOADS = [("x", 0), ("x", 1), ("w", 0, 0), "ba", ("w", 0, 1), ("w", 0, 2), ("w", 0, 3), "c",
-         ("w", 1, None), ("w", 2, 0), "bb", ("w", 2, 1)]
+LOADS = [("x", 0), ("x", 1), ("w", 0, None), "c", ("w", 1, None), ("w", 2, None)]
 LT = 3
 LQ = 1
 HEAD = 8
-COMB_AT = 2
-QC_AT = 3
+COMB_AT = 3
+BIAS_AT = 0
+QC_AT = 5
 WRAW_BUFS, WG_BUFS, WQ_BUFS, YQ_BUFS, O_BUFS = 3, 6, 8, 6, 3
 
 
@@ -57,15 +57,19 @@ def tile_expertschoosemaskedexpand_kernel(
             x_sb.append(const.tile([P, 2, E * I], BF16, name="x_sb%d" % b))
             dm_sb.append(const.tile([P, 2, E * C], BF16, name="dm_sb%d" % b))
         comb_sb = const.tile([P, 2 * B, E * C], BF16, name="comb_sb")
-        bias_a = const.tile([P, 2 * OC], BF16, name="bias_a")
-        bias_b = const.tile([P, O - 2 * OC], BF16, name="bias_b")
+        bias_row = const.tile([P, O], BF16, name="bias_row")
+        ones = const.tile([P, P], BF16, name="ones")
+        bias_bc = [const.tile([P, OC], BF16, name="bias_bc%d" % n) for n in range(NCH)]
+        nc.vector.memset(ones[:], 1.0)
+        nc.vector.memset(bias_row[:], 0.0)
+        nc.scalar.dma_start(out=bias_row[0:1, :], in_=bias.rearrange("(a n) -> a n", a=1))
         wraw = {}
 
         def load_xb(b):
             nc.sync.dma_start(
-                out=dm_sb[b][:], in_=dispatch_mask[b].rearrange("(h p) e c -> p h (e c)", p=P)
+                out=dm_sb[b][:], in_=dispatch_mask[b].rearrange("(p h) e c -> p h (e c)", h=2)
             )
-            nc.sync.dma_start(out=x_sb[b][:], in_=x[b].rearrange("(h p) f -> p h f", p=P))
+            nc.sync.dma_start(out=x_sb[b][:], in_=x[b].rearrange("(p h) f -> p h f", h=2))
 
         def load_w(n, part=None):
             parts = PARTS[n] if n < len(PARTS) else 1
@@ -84,14 +88,10 @@ def tile_expertschoosemaskedexpand_kernel(
             return rows.bitcast(F32)
 
         def load(tok):
-            if tok == "ba":
-                nc.sync.dma_start(out=bias_a[:], in_=bias[0 : 2 * OC].partition_broadcast(P))
-            elif tok == "bb":
-                nc.sync.dma_start(out=bias_b[:], in_=bias[2 * OC : O].partition_broadcast(P))
-            elif tok == "c":
+            if tok == "c":
                 nc.sync.dma_start(
-                    out=comb_sb[:],
-                    in_=combine_array.rearrange("b (h p) e c -> p (b h) (e c)", p=P),
+                    out=comb_sb[:].rearrange("p (b h) k -> p b (h k)", b=B),
+                    in_=combine_array.rearrange("b (p h) e c -> p b (h e c)", h=2),
                 )
             elif tok[0] == "x":
                 load_xb(tok[1])
@@ -100,6 +100,16 @@ def tile_expertschoosemaskedexpand_kernel(
 
         for tok in LOADS:
             load(tok)
+
+        def bias_spread(n, eng):
+            bp = ps_o.tile([P, OC], F32, name="bp", tag="op")
+            nc.tensor.matmul(
+                out=bp[:], lhsT=ones[:], rhs=bias_row[:, n * OC : (n + 1) * OC], start=True, stop=True
+            )
+            if eng == 0:
+                nc.scalar.copy(out=bias_bc[n][:], in_=bp[:])
+            else:
+                nc.vector.tensor_copy(out=bias_bc[n][:], in_=bp[:])
 
         xg_t, x_codes, x_scales = {}, {}, {}
 
@@ -204,11 +214,7 @@ def tile_expertschoosemaskedexpand_kernel(
         def ye(n, b, s):
             if s == 0:
                 yg_t[(n, b)] = yg_pool.tile([P, OC, E], BF16, name="yg", tag="yg", align_bytes=64)
-            if n < 2:
-                bsrc = bias_a[:, n * OC : (n + 1) * OC]
-            else:
-                bsrc = bias_b[:, (n - 2) * OC : (n - 1) * OC]
-            bcol = bsrc.rearrange("c (p j) -> c j p", j=4)[:, s, :]
+            bcol = bias_bc[n][:].rearrange("c (p j) -> c j p", j=4)[:, s, :]
             nc.vector.tensor_tensor(
                 out=yg_t[(n, b)][:, s * P : (s + 1) * P, :].rearrange("c (g i) e -> c g e i", i=4),
                 in0=yp_t[(n, b, s)][:].rearrange("c e (g i) -> c g e i", i=4),
@@ -255,7 +261,7 @@ def tile_expertschoosemaskedexpand_kernel(
 
         def store(n, b):
             nc.scalar.dma_start(
-                out=out[b, :, n * OC : (n + 1) * OC].rearrange("(h p) o -> p h o", p=P),
+                out=out[b, :, n * OC : (n + 1) * OC].rearrange("(p h) o -> p h o", h=2),
                 in_=o_t[(n, b)][:],
             )
 
@@ -316,6 +322,8 @@ def tile_expertschoosemaskedexpand_kernel(
             for b in range(B):
                 if a <= COMB_AT + b < z:
                     comb_t(b)
+            if a >= BIAS_AT and z == a + 1 and 2 + a - BIAS_AT < NCH:
+                bias_spread(2 + a - BIAS_AT, 0)
             t_upto(z + LT + more)
             while seen[0] < nu:
                 v_step()
@@ -328,6 +336,8 @@ def tile_expertschoosemaskedexpand_kernel(
                 if half == 1:
                     s3_todo.extend([(n, b, hh) for b in range(B) for hh in range(2)])
 
+        bias_spread(0, 1)
+        bias_spread(1, 1)
         for b in range(B):
             for e in range(E):
                 step1(b, e)

@@ -9,6 +9,7 @@ U32 = mybir.dt.uint32
 U8 = mybir.dt.uint8
 FP8X4 = mybir.dt.float8_e4m3fn_x4
 ADD = mybir.AluOpType.add
+MULT = mybir.AluOpType.mult
 
 B, T, E, C, I, O = 2, 256, 4, 128, 512, 4096
 P = 128
@@ -21,9 +22,10 @@ PARTS = [4, 4, 2]
 LOADS = [("x", 0), ("x", 1), ("w", 0, None), "c", ("w", 1, None), ("w", 2, None)]
 LT = 3
 LQ = 1
-HEAD = 8
+HEAD = 32
 COMB_AT = 3
 BIAS_AT = 0
+BMAJOR = 1
 QC_AT = 5
 WRAW_BUFS, WG_BUFS, WQ_BUFS, YQ_BUFS, O_BUFS = 3, 6, 8, 6, 3
 
@@ -57,12 +59,12 @@ def tile_expertschoosemaskedexpand_kernel(
             x_sb.append(const.tile([P, 2, E * I], BF16, name="x_sb%d" % b))
             dm_sb.append(const.tile([P, 2, E * C], BF16, name="dm_sb%d" % b))
         comb_sb = const.tile([P, 2 * B, E * C], BF16, name="comb_sb")
-        bias_row = const.tile([P, O], BF16, name="bias_row")
+        bias_sb = const.tile([P, O // P], BF16, name="bias_sb")
         ones = const.tile([P, P], BF16, name="ones")
+        bias_dg = [const.tile([P, OC // 32, 32], BF16, name="bias_dg%d" % n) for n in range(NCH)]
         bias_bc = [const.tile([P, OC], BF16, name="bias_bc%d" % n) for n in range(NCH)]
         nc.vector.memset(ones[:], 1.0)
-        nc.vector.memset(bias_row[:], 0.0)
-        nc.scalar.dma_start(out=bias_row[0:1, :], in_=bias.rearrange("(a n) -> a n", a=1))
+        nc.sync.dma_start(out=bias_sb[:], in_=bias.rearrange("(k j) -> k j", j=O // P))
         wraw = {}
 
         def load_xb(b):
@@ -101,15 +103,25 @@ def tile_expertschoosemaskedexpand_kernel(
         for tok in LOADS:
             load(tok)
 
-        def bias_spread(n, eng):
+        def bias_diag(n):
+            g = OC // 32
+            nc.vector.tensor_tensor(
+                out=bias_dg[n][:],
+                in0=bias_sb[:].unsqueeze(1).to_broadcast([P, g, 32]),
+                in1=ident_b[:, n * g : (n + 1) * g].unsqueeze(2).to_broadcast([P, g, 32]),
+                op=MULT,
+            )
+
+        def bias_spread(n):
             bp = ps_o.tile([P, OC], F32, name="bp", tag="op")
             nc.tensor.matmul(
-                out=bp[:], lhsT=ones[:], rhs=bias_row[:, n * OC : (n + 1) * OC], start=True, stop=True
+                out=bp[:],
+                lhsT=ones[:],
+                rhs=bias_dg[n][:].rearrange("k g j -> k (g j)"),
+                start=True,
+                stop=True,
             )
-            if eng == 0:
-                nc.scalar.copy(out=bias_bc[n][:], in_=bp[:])
-            else:
-                nc.vector.tensor_copy(out=bias_bc[n][:], in_=bp[:])
+            nc.scalar.copy(out=bias_bc[n][:], in_=bp[:])
 
         xg_t, x_codes, x_scales = {}, {}, {}
 
@@ -265,6 +277,12 @@ def tile_expertschoosemaskedexpand_kernel(
                 in_=o_t[(n, b)][:],
             )
 
+        def store_half(n, b, hh):
+            nc.sync.dma_start(
+                out=out[b, :, n * OC : (n + 1) * OC].rearrange("(p h) o -> p h o", h=2)[:, hh, :],
+                in_=o_t[(n, b)][:, hh, :],
+            )
+
         NSL = 4 * NCH
         state = {"t": 0, "q": 0, "w": 3, "s3": 0}
         s3_todo = []
@@ -299,9 +317,14 @@ def tile_expertschoosemaskedexpand_kernel(
                     if hh == 1:
                         store(n, b)
 
-        def group(a, z):
+        def group(a, z, only_b=None):
             more = 0 if z < HEAD else 1
-            units = [(sl // 4, b, sl % 4) for sl in range(a, z) for b in range(B)]
+            if only_b is None:
+                units = [(sl // 4, b, sl % 4) for sl in range(a, z) for b in range(B)]
+            else:
+                units = [(sl // 4, only_b, sl % 4) for sl in range(a, z)]
+                t_upto(z)
+                q_upto(z)
             nu = len(units)
             q_at = nu // 2 if nu > 2 else 0
             seen = [0]
@@ -309,13 +332,15 @@ def tile_expertschoosemaskedexpand_kernel(
             def v_step():
                 if seen[0] == q_at:
                     q_upto(z + LQ + more)
+                    if only_b is not None:
+                        qy(units[0][0], only_b, 0)
                 ye(*units[seen[0]])
                 seen[0] += 1
 
             for i, un in enumerate(units):
                 if i == min(YP_BUFS, nu - 1) and a > QC_AT:
                     backlog = len(s3_todo) - state["s3"]
-                    s3_some((z - a) + (1 if backlog > 4 else 0))
+                    s3_some((2 if only_b is not None else z - a) + (1 if backlog > 4 else 0))
                 if i >= YP_BUFS:
                     v_step()
                 s2_pe(*un)
@@ -323,21 +348,26 @@ def tile_expertschoosemaskedexpand_kernel(
                 if a <= COMB_AT + b < z:
                     comb_t(b)
             if a >= BIAS_AT and z == a + 1 and 2 + a - BIAS_AT < NCH:
-                bias_spread(2 + a - BIAS_AT, 0)
+                bias_spread(2 + a - BIAS_AT)
             t_upto(z + LT + more)
             while seen[0] < nu:
                 v_step()
             if a <= QC_AT < z:
                 qc()
-            if z % 2 == 0:
+            if only_b is not None:
+                qy(units[0][0], only_b, 1)
+                s3_todo.extend([(units[0][0], only_b, hh) for hh in range(2)])
+            elif z % 2 == 0:
                 n, half = (z - 1) // 4, ((z - 1) % 4) // 2
                 for b in range(B):
                     qy(n, b, half)
                 if half == 1:
                     s3_todo.extend([(n, b, hh) for b in range(B) for hh in range(2)])
 
-        bias_spread(0, 1)
-        bias_spread(1, 1)
+        for n in range(NCH):
+            bias_diag(n)
+            if n < 2:
+                bias_spread(n)
         for b in range(B):
             for e in range(E):
                 step1(b, e)
@@ -345,20 +375,22 @@ def tile_expertschoosemaskedexpand_kernel(
         t_upto(LT)
         q_upto(LQ)
         a = 0
-        while a < NSL:
+        while a < NSL - 4 * BMAJOR:
             z = a + (1 if a < HEAD else 2)
             group(a, z)
             a = z
+        while a < NSL:
+            for b in range(B):
+                group(a, a + 4, b)
+            a += 4
         rest = s3_todo[state["s3"] :]
         for i, (n, b, hh) in enumerate(rest):
             if i >= OP_BUFS:
                 pn, pb, ph = rest[i - OP_BUFS]
                 o_ev(pn, pb, ph, (i - OP_BUFS) % 2)
-                if ph == 1:
-                    store(pn, pb)
+                store_half(pn, pb, ph)
             s3_pe(n, b, hh)
         for i in range(max(0, len(rest) - OP_BUFS), len(rest)):
             n, b, hh = rest[i]
             o_ev(n, b, hh, i % 2)
-            if hh == 1:
-                store(n, b)
+            store_half(n, b, hh)

@@ -25,6 +25,9 @@ LQ = 1
 HEAD = 32
 COMB_AT = 3
 BIAS_AT = 0
+QY_LATE = True
+S3_LAG = 1
+RAMP = []
 BMAJOR = 1
 QC_AT = 5
 WRAW_BUFS, WG_BUFS, WQ_BUFS, YQ_BUFS, O_BUFS = 3, 6, 8, 6, 3
@@ -284,7 +287,7 @@ def tile_expertschoosemaskedexpand_kernel(
             )
 
         NSL = 4 * NCH
-        state = {"t": 0, "q": 0, "w": 3, "s3": 0}
+        state = {"t": 0, "q": 0, "w": 3, "s3": 0, "qy": 0}
         s3_todo = []
 
         def t_upto(want):
@@ -307,18 +310,29 @@ def tile_expertschoosemaskedexpand_kernel(
                 qw(state["q"] // 4, state["q"] % 4)
                 state["q"] += 1
 
-        def s3_some(count):
+        def s3_some(count, now):
             for j in range(count):
-                if state["s3"] < len(s3_todo):
-                    n, b, hh = s3_todo[state["s3"]]
+                if state["s3"] < len(s3_todo) and s3_todo[state["s3"]][3] <= now:
+                    n, b, hh = s3_todo[state["s3"]][:3]
                     state["s3"] += 1
                     s3_pe(n, b, hh)
                     o_ev(n, b, hh, 0)
                     if hh == 1:
                         store(n, b)
 
+        qy_todo = []
+
+        def qy_due():
+            if len(qy_todo) > state["qy"]:
+                n, half, z = qy_todo[state["qy"] : state["qy"] + 3]
+                state["qy"] += 3
+                for b in range(B):
+                    qy(n, b, half)
+                if half == 1:
+                    s3_todo.extend([(n, b, hh, z + S3_LAG) for b in range(B) for hh in range(2)])
+
         def group(a, z, only_b=None):
-            more = 0 if z < HEAD else 1
+            more = sum(1 for r in RAMP if z >= r)
             if only_b is None:
                 units = [(sl // 4, b, sl % 4) for sl in range(a, z) for b in range(B)]
             else:
@@ -332,15 +346,18 @@ def tile_expertschoosemaskedexpand_kernel(
             def v_step():
                 if seen[0] == q_at:
                     q_upto(z + LQ + more)
+                    qy_due()
                     if only_b is not None:
                         qy(units[0][0], only_b, 0)
                 ye(*units[seen[0]])
                 seen[0] += 1
 
             for i, un in enumerate(units):
-                if i == min(YP_BUFS, nu - 1) and a > QC_AT:
+                if only_b is not None:
+                    s3_some(1, NSL)
+                elif i == min(YP_BUFS, nu - 1) and a > QC_AT:
                     backlog = len(s3_todo) - state["s3"]
-                    s3_some((2 if only_b is not None else z - a) + (1 if backlog > 4 else 0))
+                    s3_some(z - a + (1 if backlog > 4 else 0), a)
                 if i >= YP_BUFS:
                     v_step()
                 s2_pe(*un)
@@ -356,13 +373,13 @@ def tile_expertschoosemaskedexpand_kernel(
                 qc()
             if only_b is not None:
                 qy(units[0][0], only_b, 1)
-                s3_todo.extend([(units[0][0], only_b, hh) for hh in range(2)])
+                s3_todo.extend([(units[0][0], only_b, hh, 0) for hh in range(2)])
             elif z % 2 == 0:
-                n, half = (z - 1) // 4, ((z - 1) % 4) // 2
-                for b in range(B):
-                    qy(n, b, half)
-                if half == 1:
-                    s3_todo.extend([(n, b, hh) for b in range(B) for hh in range(2)])
+                qy_todo.append((z - 1) // 4)
+                qy_todo.append(((z - 1) % 4) // 2)
+                qy_todo.append(z)
+                if not QY_LATE:
+                    qy_due()
 
         for n in range(NCH):
             bias_diag(n)
@@ -383,7 +400,7 @@ def tile_expertschoosemaskedexpand_kernel(
             for b in range(B):
                 group(a, a + 4, b)
             a += 4
-        rest = s3_todo[state["s3"] :]
+        rest = [td[:3] for td in s3_todo[state["s3"] :]]
         for i, (n, b, hh) in enumerate(rest):
             if i >= OP_BUFS:
                 pn, pb, ph = rest[i - OP_BUFS]

@@ -16,7 +16,7 @@ P = 128
 OC = 512
 NCH = O // OC
 FLOPS = 2 * B * E * C * I * T + 2 * B * E * C * I * O + 2 * B * T * E * C * O
-MANUAL = True
+MANUAL = False
 TP_BUFS, YP_BUFS, OP_BUFS = 3, 3, 2
 PARTS = [4, 4, 2]
 LOADS = [("x", 0), ("x", 1), ("w", 0, None), "c", ("w", 1, None), ("w", 2, None)]
@@ -25,9 +25,6 @@ LQ = 1
 HEAD = 32
 COMB_AT = 3
 BIAS_AT = 0
-QY_LATE = True
-S3_LAG = 1
-RAMP = []
 BMAJOR = 1
 QC_AT = 5
 WRAW_BUFS, WG_BUFS, WQ_BUFS, YQ_BUFS, O_BUFS = 3, 6, 8, 6, 3
@@ -287,7 +284,7 @@ def tile_expertschoosemaskedexpand_kernel(
             )
 
         NSL = 4 * NCH
-        state = {"t": 0, "q": 0, "w": 3, "s3": 0, "qy": 0}
+        state = {"t": 0, "q": 0, "w": 3, "s3": 0}
         s3_todo = []
 
         def t_upto(want):
@@ -310,29 +307,18 @@ def tile_expertschoosemaskedexpand_kernel(
                 qw(state["q"] // 4, state["q"] % 4)
                 state["q"] += 1
 
-        def s3_some(count, now):
+        def s3_some(count):
             for j in range(count):
-                if state["s3"] < len(s3_todo) and s3_todo[state["s3"]][3] <= now:
-                    n, b, hh = s3_todo[state["s3"]][:3]
+                if state["s3"] < len(s3_todo):
+                    n, b, hh = s3_todo[state["s3"]]
                     state["s3"] += 1
                     s3_pe(n, b, hh)
                     o_ev(n, b, hh, 0)
                     if hh == 1:
                         store(n, b)
 
-        qy_todo = []
-
-        def qy_due():
-            if len(qy_todo) > state["qy"]:
-                n, half, z = qy_todo[state["qy"] : state["qy"] + 3]
-                state["qy"] += 3
-                for b in range(B):
-                    qy(n, b, half)
-                if half == 1:
-                    s3_todo.extend([(n, b, hh, z + S3_LAG) for b in range(B) for hh in range(2)])
-
         def group(a, z, only_b=None):
-            more = sum(1 for r in RAMP if z >= r)
+            more = 0 if z < HEAD else 1
             if only_b is None:
                 units = [(sl // 4, b, sl % 4) for sl in range(a, z) for b in range(B)]
             else:
@@ -346,18 +332,15 @@ def tile_expertschoosemaskedexpand_kernel(
             def v_step():
                 if seen[0] == q_at:
                     q_upto(z + LQ + more)
-                    qy_due()
                     if only_b is not None:
                         qy(units[0][0], only_b, 0)
                 ye(*units[seen[0]])
                 seen[0] += 1
 
             for i, un in enumerate(units):
-                if only_b is not None:
-                    s3_some(1, NSL)
-                elif i == min(YP_BUFS, nu - 1) and a > QC_AT:
+                if i == min(YP_BUFS, nu - 1) and a > QC_AT:
                     backlog = len(s3_todo) - state["s3"]
-                    s3_some(z - a + (1 if backlog > 4 else 0), a)
+                    s3_some((2 if only_b is not None else z - a) + (1 if backlog > 4 else 0))
                 if i >= YP_BUFS:
                     v_step()
                 s2_pe(*un)
@@ -373,13 +356,13 @@ def tile_expertschoosemaskedexpand_kernel(
                 qc()
             if only_b is not None:
                 qy(units[0][0], only_b, 1)
-                s3_todo.extend([(units[0][0], only_b, hh, 0) for hh in range(2)])
+                s3_todo.extend([(units[0][0], only_b, hh) for hh in range(2)])
             elif z % 2 == 0:
-                qy_todo.append((z - 1) // 4)
-                qy_todo.append(((z - 1) % 4) // 2)
-                qy_todo.append(z)
-                if not QY_LATE:
-                    qy_due()
+                n, half = (z - 1) // 4, ((z - 1) % 4) // 2
+                for b in range(B):
+                    qy(n, b, half)
+                if half == 1:
+                    s3_todo.extend([(n, b, hh) for b in range(B) for hh in range(2)])
 
         for n in range(NCH):
             bias_diag(n)
@@ -400,7 +383,7 @@ def tile_expertschoosemaskedexpand_kernel(
             for b in range(B):
                 group(a, a + 4, b)
             a += 4
-        rest = [td[:3] for td in s3_todo[state["s3"] :]]
+        rest = s3_todo[state["s3"] :]
         for i, (n, b, hh) in enumerate(rest):
             if i >= OP_BUFS:
                 pn, pb, ph = rest[i - OP_BUFS]

@@ -16,7 +16,7 @@ P = 128
 OC = 512
 NCH = O // OC
 FLOPS = 2 * B * E * C * I * T + 2 * B * E * C * I * O + 2 * B * T * E * C * O
-MANUAL = False
+MANUAL = True
 TP_BUFS, YP_BUFS, OP_BUFS = 3, 3, 2
 PARTS = [4, 4, 2]
 LOADS = [("x", 0), ("x", 1), ("w", 0, None), "c", ("w", 1, None), ("w", 2, None)]
@@ -27,7 +27,7 @@ COMB_AT = 3
 BIAS_AT = 0
 BMAJOR = 1
 QC_AT = 5
-WRAW_BUFS, WG_BUFS, WQ_BUFS, YQ_BUFS, O_BUFS = 3, 6, 8, 6, 3
+WRAW_BUFS, WG_BUFS, WQ_BUFS, YQ_BUFS, O_BUFS = 3, 6, 8, 6, 6
 
 
 def tile_expertschoosemaskedexpand_kernel(

from contextlib import ExitStack

import concourse.mybir as mybir
from concourse.masks import make_identity

F32 = mybir.dt.float32
BF16 = mybir.dt.bfloat16
U32 = mybir.dt.uint32
U8 = mybir.dt.uint8
FP8X4 = mybir.dt.float8_e4m3fn_x4
ADD = mybir.AluOpType.add
MULT = mybir.AluOpType.mult

B, T, E, C, I, O = 2, 256, 4, 128, 512, 4096
P = 128
OC = 512
NCH = O // OC
FLOPS = 2 * B * E * C * I * T + 2 * B * E * C * I * O + 2 * B * T * E * C * O
MANUAL = True
TP_BUFS, YP_BUFS, OP_BUFS = 3, 3, 2
PARTS = [4, 4, 2]
LOADS = [("x", 0), ("x", 1), ("w", 0, None), "c", ("w", 1, None), ("w", 2, None)]
LT = 3
LQ = 1
HEAD = 32
COMB_AT = 3
BIAS_AT = 0
BMAJOR = 1
QC_AT = 5
WRAW_BUFS, WG_BUFS, WQ_BUFS, YQ_BUFS, O_BUFS = 3, 6, 8, 6, 6


def tile_expertschoosemaskedexpand_kernel(
    tc, x, combine_array, dispatch_mask, weight, bias, num_experts, out
):
    nc = tc.nc
    with ExitStack() as ctx:
        const = ctx.enter_context(tc.tile_pool(name="const", bufs=1))
        wraw_pool = ctx.enter_context(tc.tile_pool(name="wraw", bufs=WRAW_BUFS))
        wg_pool = ctx.enter_context(tc.tile_pool(name="wg", bufs=WG_BUFS))
        wq_pool = ctx.enter_context(tc.tile_pool(name="wq", bufs=WQ_BUFS))
        yg_pool = ctx.enter_context(tc.tile_pool(name="yg", bufs=4))
        yq_pool = ctx.enter_context(tc.tile_pool(name="yq", bufs=YQ_BUFS))
        o_pool = ctx.enter_context(tc.tile_pool(name="osb", bufs=O_BUFS))
        ps_t = ctx.enter_context(tc.psum_pool(name="ps_t", bufs=TP_BUFS))
        ps_y = ctx.enter_context(tc.psum_pool(name="ps_y", bufs=YP_BUFS))
        ps_o = ctx.enter_context(tc.psum_pool(name="ps_o", bufs=OP_BUFS))
        if MANUAL:
            ctx.enter_context(tc.manual_schedule())

        ident_f = const.tile([P, P], F32, name="ident_f")
        make_identity(nc, ident_f[:])
        ident_b = const.tile([P, P], BF16, name="ident_b")
        make_identity(nc, ident_b[:])

        w_view = weight.rearrange("(e c p) f -> c p e f", e=E, c=NCH, p=P)
        x_sb, dm_sb = [], []
        for b in range(B):
            x_sb.append(const.tile([P, 2, E * I], BF16, name="x_sb%d" % b))
            dm_sb.append(const.tile([P, 2, E * C], BF16, name="dm_sb%d" % b))
        comb_sb = const.tile([P, 2 * B, E * C], BF16, name="comb_sb")
        bias_sb = const.tile([P, O // P], BF16, name="bias_sb")
        ones = const.tile([P, P], BF16, name="ones")
        bias_dg = [const.tile([P, OC // 32, 32], BF16, name="bias_dg%d" % n) for n in range(NCH)]
        bias_bc = [const.tile([P, OC], BF16, name="bias_bc%d" % n) for n in range(NCH)]
        nc.vector.memset(ones[:], 1.0)
        nc.sync.dma_start(out=bias_sb[:], in_=bias.rearrange("(k j) -> k j", j=O // P))
        wraw = {}

        def load_xb(b):
            nc.sync.dma_start(
                out=dm_sb[b][:], in_=dispatch_mask[b].rearrange("(p h) e c -> p h (e c)", h=2)
            )
            nc.sync.dma_start(out=x_sb[b][:], in_=x[b].rearrange("(p h) f -> p h f", h=2))

        def load_w(n, part=None):
            parts = PARTS[n] if n < len(PARTS) else 1
            per = 4 // parts
            if part is None or part == 0:
                wraw[n] = (wraw_pool.tile([P, parts, E, per * I], BF16, name="wr", tag="wr"), per)
            wr = wraw[n][0]
            for g in range(parts) if part is None else [part]:
                nc.sync.dma_start(
                    out=wr[:, g], in_=w_view[n][:, :, g * per * I : (g + 1) * per * I]
                )

        def w_words(n, s, e):
            wr, per = wraw[n]
            rows = wr[:, s // per, e, (s % per) * I : (s % per + 1) * I]
            return rows.bitcast(F32)

        def load(tok):
            if tok == "c":
                nc.sync.dma_start(
                    out=comb_sb[:].rearrange("p (b h) k -> p b (h k)", b=B),
                    in_=combine_array.rearrange("b (p h) e c -> p b (h e c)", h=2),
                )
            elif tok[0] == "x":
                load_xb(tok[1])
            else:
                load_w(tok[1], tok[2])

        for tok in LOADS:
            load(tok)

        def bias_diag(n):
            g = OC // 32
            nc.vector.tensor_tensor(
                out=bias_dg[n][:],
                in0=bias_sb[:].unsqueeze(1).to_broadcast([P, g, 32]),
                in1=ident_b[:, n * g : (n + 1) * g].unsqueeze(2).to_broadcast([P, g, 32]),
                op=MULT,
            )

        def bias_spread(n):
            bp = ps_o.tile([P, OC], F32, name="bp", tag="op")
            nc.tensor.matmul(
                out=bp[:],
                lhsT=ones[:],
                rhs=bias_dg[n][:].rearrange("k g j -> k (g j)"),
                start=True,
                stop=True,
            )
            nc.scalar.copy(out=bias_bc[n][:], in_=bp[:])

        xg_t, x_codes, x_scales = {}, {}, {}

        def step1(b, e):
            if e == 0:
                xg_t[b] = const.tile([P, E, C, 4], BF16, name="xg%d" % b, align_bytes=64)
            xp = ps_y.tile([P, 4, C], F32, name="xp", tag="yp")
            for u in range(2):
                for w in range(2):
                    for h in range(2):
                        cols = x_sb[b][:, h, e * I : (e + 1) * I].rearrange(
                            "t (u q w) -> t u w q", u=2, w=2
                        )
                        nc.tensor.matmul(
                            out=xp[:, 2 * u + w, :],
                            lhsT=cols[:, u, w, :],
                            rhs=dm_sb[b][:, h, e * C : (e + 1) * C],
                            start=(h == 0),
                            stop=(h == 1),
                        )
            nc.scalar.copy(out=xg_t[b][:, e], in_=xp[:].rearrange("q t c -> q c t"))

        def qx(b):
            xc = const.tile([P, E * C], U32, name="xc%d" % b, align_bytes=64)
            xs = const.tile([P, E * C], U8, name="xs%d" % b, align_bytes=64)
            nc.vector.quantize_mx(
                out=xc[:].bitcast(FP8X4),
                scales=xs[:],
                in_=xg_t[b][:].rearrange("q e c t -> q (e c t)"),
            )
            x_codes[b] = xc
            x_scales[b] = xs

        cg = const.tile([P, 2 * B, P, 4], BF16, name="cg", align_bytes=64)
        c_codes = const.tile([P, 2 * B * P], U32, name="c_codes", align_bytes=64)
        c_scales = const.tile([P, 2 * B * P], U8, name="c_scales", align_bytes=64)

        def comb_t(b):
            cp = ps_o.tile([P, 2, E, P], BF16, name="cp", tag="op")
            for hh in range(2):
                for e in range(E):
                    nc.tensor.transpose(
                        cp[:, hh, e, :], comb_sb[:, 2 * b + hh, e * C : (e + 1) * C], ident_b[:]
                    )
            nc.scalar.copy(
                out=cg[:, 2 * b : 2 * b + 2], in_=cp[:].rearrange("c g e t -> c g t e")
            )

        def qc():
            nc.vector.quantize_mx(
                out=c_codes[:].bitcast(FP8X4),
                scales=c_scales[:],
                in_=cg[:].rearrange("c g t e -> c (g t e)"),
            )

        tp_t, wg_t, w_codes, w_scales = {}, {}, {}, {}

        def t_pe(n, s, ep):
            tp = ps_t.tile([P, 2, 2 * P], F32, name="tp", tag="tp")
            for el in range(2):
                words = w_words(n, s, 2 * ep + el)
                for u in range(2):
                    nc.tensor.transpose(
                        tp[:, u, el * P : (el + 1) * P], words[:, u * P : (u + 1) * P], ident_f[:]
                    )
            tp_t[(n, s, ep)] = tp

        def t_ev(n, s, ep):
            if ep == 0:
                wg_t[(n, s)] = wg_pool.tile(
                    [P, 4 * E * P], BF16, name="wg", tag="wg", align_bytes=64
                )
            wgf = wg_t[(n, s)][:].bitcast(F32).rearrange("q (n u) -> q n u", u=2)
            nc.scalar.copy(
                out=wgf[:, ep * 2 * P : (ep + 1) * 2 * P, :],
                in_=tp_t[(n, s, ep)][:].rearrange("q u n -> q n u"),
            )

        def qw(n, s):
            wc = wq_pool.tile([P, E * P], U32, name="wc", tag="wc", align_bytes=64)
            ws = wq_pool.tile([P, E * P], U8, name="ws", tag="ws", align_bytes=64)
            nc.vector.quantize_mx(out=wc[:].bitcast(FP8X4), scales=ws[:], in_=wg_t[(n, s)][:])
            w_codes[(n, s)] = wc
            w_scales[(n, s)] = ws

        yp_t, yg_t, y_codes, y_scales, op_t, o_t = {}, {}, {}, {}, {}, {}

        def s2_pe(n, b, s):
            yp = ps_y.tile([P, E, P], F32, name="yp", tag="yp")
            for e in range(E):
                nc.tensor.matmul_mx(
                    out=yp[:, e, :],
                    lhsT=x_codes[b][:, e * C : (e + 1) * C].bitcast(FP8X4),
                    lhsT_scale=x_scales[b][:, e * C : (e + 1) * C],
                    rhs=w_codes[(n, s)][:, e * P : (e + 1) * P].bitcast(FP8X4),
                    rhs_scale=w_scales[(n, s)][:, e * P : (e + 1) * P],
                    start=True,
                    stop=True,
                )
            yp_t[(n, b, s)] = yp

        def ye(n, b, s):
            if s == 0:
                yg_t[(n, b)] = yg_pool.tile([P, OC, E], BF16, name="yg", tag="yg", align_bytes=64)
            bcol = bias_bc[n][:].rearrange("c (p j) -> c j p", j=4)[:, s, :]
            nc.vector.tensor_tensor(
                out=yg_t[(n, b)][:, s * P : (s + 1) * P, :].rearrange("c (g i) e -> c g e i", i=4),
                in0=yp_t[(n, b, s)][:].rearrange("c e (g i) -> c g e i", i=4),
                in1=bcol.rearrange("c (g i) -> c g i", i=4)
                .unsqueeze(2)
                .to_broadcast([P, P // 4, E, 4]),
                op=ADD,
            )

        def qy(n, b, half):
            if half == 0:
                y_codes[(n, b)] = yq_pool.tile([P, OC], U32, name="yc", tag="yc", align_bytes=64)
                y_scales[(n, b)] = yq_pool.tile([P, OC], U8, name="ys", tag="ys", align_bytes=64)
            cols = slice(half * 2 * P, (half + 1) * 2 * P)
            nc.vector.quantize_mx(
                out=y_codes[(n, b)][:, cols].bitcast(FP8X4),
                scales=y_scales[(n, b)][:, cols],
                in_=yg_t[(n, b)][:, cols, :].rearrange("c n e -> c (n e)"),
            )

        def s3_pe(n, b, h):
            bh = 2 * b + h
            op = ps_o.tile([P, OC], F32, name="op", tag="op")
            nc.tensor.matmul_mx(
                out=op[:],
                lhsT=c_codes[:, bh * P : (bh + 1) * P].bitcast(FP8X4),
                lhsT_scale=c_scales[:, bh * P : (bh + 1) * P],
                rhs=y_codes[(n, b)][:].bitcast(FP8X4),
                rhs_scale=y_scales[(n, b)][:],
                start=True,
                stop=True,
            )
            op_t[(n, b, h)] = op

        def o_ev(n, b, h, eng):
            if h == 0:
                o_t[(n, b)] = o_pool.tile([P, 2, OC], F32, name="osb", tag="osb")
            dst = o_t[(n, b)][:, h, :].rearrange("t (p s) -> t p s", s=4)
            src = op_t[(n, b, h)][:].rearrange("t (s p) -> t p s", s=4)
            if eng == 0:
                nc.scalar.copy(out=dst, in_=src)
            else:
                nc.vector.tensor_copy(out=dst, in_=src)

        def store(n, b):
            nc.scalar.dma_start(
                out=out[b, :, n * OC : (n + 1) * OC].rearrange("(p h) o -> p h o", h=2),
                in_=o_t[(n, b)][:],
            )

        def store_half(n, b, hh):
            nc.sync.dma_start(
                out=out[b, :, n * OC : (n + 1) * OC].rearrange("(p h) o -> p h o", h=2)[:, hh, :],
                in_=o_t[(n, b)][:, hh, :],
            )

        NSL = 4 * NCH
        state = {"t": 0, "q": 0, "w": 3, "s3": 0}
        s3_todo = []

        def t_upto(want):
            want = min(NSL, want)
            banks = [(sl // 4, sl % 4, ep) for sl in range(state["t"], want) for ep in range(2)]
            for i, bk in enumerate(banks):
                if i >= TP_BUFS:
                    t_ev(*banks[i - TP_BUFS])
                if bk[1] == 0 and bk[2] == 0 and bk[0] >= 1 and state["w"] < NCH:
                    load_w(state["w"])
                    state["w"] += 1
                t_pe(*bk)
            for bk in banks[max(0, len(banks) - TP_BUFS) :]:
                t_ev(*bk)
            state["t"] = max(state["t"], want)

        def q_upto(want):
            want = min(NSL, want)
            while state["q"] < want:
                qw(state["q"] // 4, state["q"] % 4)
                state["q"] += 1

        def s3_some(count):
            for j in range(count):
                if state["s3"] < len(s3_todo):
                    n, b, hh = s3_todo[state["s3"]]
                    state["s3"] += 1
                    s3_pe(n, b, hh)
                    o_ev(n, b, hh, 0)
                    if hh == 1:
                        store(n, b)

        def group(a, z, only_b=None):
            more = 0 if z < HEAD else 1
            if only_b is None:
                units = [(sl // 4, b, sl % 4) for sl in range(a, z) for b in range(B)]
            else:
                units = [(sl // 4, only_b, sl % 4) for sl in range(a, z)]
                t_upto(z)
                q_upto(z)
            nu = len(units)
            q_at = nu // 2 if nu > 2 else 0
            seen = [0]

            def v_step():
                if seen[0] == q_at:
                    q_upto(z + LQ + more)
                    if only_b is not None:
                        qy(units[0][0], only_b, 0)
                ye(*units[seen[0]])
                seen[0] += 1

            for i, un in enumerate(units):
                if i == min(YP_BUFS, nu - 1) and a > QC_AT:
                    backlog = len(s3_todo) - state["s3"]
                    s3_some((2 if only_b is not None else z - a) + (1 if backlog > 4 else 0))
                if i >= YP_BUFS:
                    v_step()
                s2_pe(*un)
            for b in range(B):
                if a <= COMB_AT + b < z:
                    comb_t(b)
            if a >= BIAS_AT and z == a + 1 and 2 + a - BIAS_AT < NCH:
                bias_spread(2 + a - BIAS_AT)
            t_upto(z + LT + more)
            while seen[0] < nu:
                v_step()
            if a <= QC_AT < z:
                qc()
            if only_b is not None:
                qy(units[0][0], only_b, 1)
                s3_todo.extend([(units[0][0], only_b, hh) for hh in range(2)])
            elif z % 2 == 0:
                n, half = (z - 1) // 4, ((z - 1) % 4) // 2
                for b in range(B):
                    qy(n, b, half)
                if half == 1:
                    s3_todo.extend([(n, b, hh) for b in range(B) for hh in range(2)])

        for n in range(NCH):
            bias_diag(n)
            if n < 2:
                bias_spread(n)
        for b in range(B):
            for e in range(E):
                step1(b, e)
            qx(b)
        t_upto(LT)
        q_upto(LQ)
        a = 0
        while a < NSL - 4 * BMAJOR:
            z = a + (1 if a < HEAD else 2)
            group(a, z)
            a = z
        while a < NSL:
            for b in range(B):
                group(a, a + 4, b)
            a += 4
        rest = s3_todo[state["s3"] :]
        for i, (n, b, hh) in enumerate(rest):
            if i >= OP_BUFS:
                pn, pb, ph = rest[i - OP_BUFS]
                o_ev(pn, pb, ph, (i - OP_BUFS) % 2)
                store_half(pn, pb, ph)
            s3_pe(n, b, hh)
        for i in range(max(0, len(rest) - OP_BUFS), len(rest)):
            n, b, hh = rest[i]
            o_ev(n, b, hh, i % 2)
            store_half(n, b, hh)
